import numpy as np
import ml_dtypes


def mxq(x, axis, fmt="e4m3"):
    dtype, down = {"e4m3": (ml_dtypes.float8_e4m3fn, 7), "e5m2": (ml_dtypes.float8_e5m2, 14)}[fmt]
    v = np.moveaxis(np.asarray(x, np.float32).astype(ml_dtypes.bfloat16).astype(np.float64), axis, -1)
    blocks = v.reshape(v.shape[:-1] + (-1, 32))
    amax = np.abs(blocks).max(-1, keepdims=True)
    byte = np.maximum(np.where(amax > 0, np.frexp(amax)[1] - 1 + 127, 0) - down, 1)
    scale = np.exp2(byte - 127.0)
    codes = (blocks / scale).astype(np.float32).astype(dtype).astype(np.float64)
    return np.moveaxis((codes * scale).reshape(v.shape), -1, axis)


WIDE = False


def mx_kscale(k):
    if not WIDE:
        return np.ones(k)
    levels = np.array([20, -20, 10, -10, 0])
    a = np.random.permutation(np.resize(levels, k // 512 * 4)).reshape(k // 512, 4)
    idx = np.arange(k)
    return np.exp2(a[idx // 512, idx % 128 // 32])


BF16 = ml_dtypes.bfloat16


def bf(x):
    return np.asarray(x, np.float32).astype(BF16)


def f64(x):
    return np.asarray(x).astype(np.float64)


B, S, I, O = 4, 1024, 1024, 1024
T = B * S
W_MAG = 2.0 ** -6


def draw_weight():
    return np.where(np.random.standard_normal((O, I)) < 0.0, -W_MAG, W_MAG)


def setup_inputs():
    s = mx_kscale(T).reshape(B, S, 1)
    x = np.random.standard_normal((B, S, I)) * s
    w = draw_weight()
    g = np.random.standard_normal((B, S, O)) * np.exp2(np.random.randint(-12, 1, (B, S, 1))) * 0.25 / s
    return {"x": bf(x), "weight": bf(w), "grad_out": bf(g)}


def reference(x, weight, grad_out):
    x2 = f64(x).reshape(T, I)
    g2 = f64(grad_out).reshape(T, O)
    return mxq(g2, 0, "e5m2").T @ mxq(x2, 0, "e4m3")

@@ -1,0 +1,192 @@
+import concourse.mybir as mybir
+
+FLOPS = 2 * 4096 * 1024 * 1024
+BYTES = 2 * 4096 * 1024 * 2 + 1024 * 1024 * 4
+
+BF16 = mybir.dt.bfloat16
+F32 = mybir.dt.float32
+U32 = mybir.dt.uint32
+U8 = mybir.dt.uint8
+E4M3 = mybir.dt.float8_e4m3fn_x4
+E5M2 = mybir.dt.float8_e5m2_x4
+
+P = 128
+PACK = 4
+K_PASS = P * PACK
+TOKENS = 4096
+CHUNKS = TOKENS // K_PASS
+HALF = 512
+G_SPLIT = 224
+X_BUFS = 6
+G_BUFS = 8
+C_MAJOR = 4
+
+
+def tile_bitlinear_t_kernel(tc, x, weight, grad_out, out):
+    nc = tc.nc
+    xf = x.flatten_outer_dims()
+    gf = grad_out.flatten_outer_dims()
+
+    with tc.tile_pool(name="keep", bufs=1) as keep, tc.tile_pool(name="raw", bufs=1) as raw, tc.tile_pool(
+        name="stage", bufs=1
+    ) as stage, tc.psum_pool(name="psum", bufs=1) as psum:
+        x_codes = keep.tile([P, CHUNKS, 2 * HALF], U32, align_bytes=64)
+        x_scales = keep.tile([P, CHUNKS, 2 * HALF], U8, align_bytes=64)
+        g_codes = keep.tile([P, 2 * CHUNKS, HALF], U32, align_bytes=64)
+        g_scales = keep.tile([P, 2 * CHUNKS, HALF], U8, align_bytes=64)
+
+        order = []
+        for c in range(CHUNKS):
+            order.append(("g", c))
+            order.append(("x", c))
+        for c in range(CHUNKS):
+            order.append(("g", CHUNKS + c))
+        state = {"next": 0, "x_made": 0, "x_done": 0, "g_made": 0, "g_done": 0}
+        raw_tiles = {}
+
+        def emit_loads():
+            while state["next"] < len(order):
+                kind, c = order[state["next"]]
+                if kind == "x":
+                    if state["x_made"] - state["x_done"] >= X_BUFS:
+                        return
+                    t = raw.tile([P, PACK, 2 * HALF], BF16, tag="xraw", bufs=X_BUFS, name="xraw")
+                    rows = xf[c * K_PASS : (c + 1) * K_PASS, :]
+                    state["x_made"] += 1
+                else:
+                    if state["g_made"] - state["g_done"] >= G_BUFS:
+                        return
+                    t = raw.tile([P, PACK, HALF], BF16, tag="graw", bufs=G_BUFS, name="graw")
+                    cc = c % CHUNKS
+                    h = c // CHUNKS
+                    rows = gf[cc * K_PASS : (cc + 1) * K_PASS, h * HALF : (h + 1) * HALF]
+                    state["g_made"] += 1
+                nc.sync.dma_start(out=t[:], in_=rows.rearrange("(p j) w -> p j w", j=PACK))
+                raw_tiles[(kind, c)] = t
+                state["next"] += 1
+
+        def regroup(eng, dst, src):
+            d = dst.rearrange("p (c i) t -> p c t i", i=4)
+            s = src.rearrange("p t (c i) -> p c t i", i=4)
+            if eng == "v":
+                nc.vector.tensor_copy(out=d, in_=s)
+            else:
+                nc.scalar.copy(out=d, in_=s)
+
+        def new_grouped():
+            grouped = stage.tile([P, HALF, PACK], BF16, tag="grouped", bufs=6, align_bytes=64, name="grouped")
+            return grouped
+
+        def quantise(grouped, codes, scales, fmt):
+            nc.vector.quantize_mx(
+                out=codes.bitcast(fmt), scales=scales, in_=grouped[:].rearrange("p w j -> p (w j)")
+            )
+
+        def quantise_x(grouped, c, n):
+            cols = slice(n * HALF, (n + 1) * HALF)
+            quantise(grouped, x_codes[:, c, cols], x_scales[:, c, cols], E4M3)
+
+        def quantise_g(grouped, u):
+            quantise(grouped, g_codes[:, u, :], g_scales[:, u, :], E5M2)
+
+        def mx_pass(acc, u, m, c, n, start, stop):
+            mc = slice(m * P, (m + 1) * P)
+            ncols = slice(n * HALF, (n + 1) * HALF)
+            nc.tensor.matmul_mx(
+                out=acc[:],
+                lhsT=g_codes[:, u, mc].bitcast(E5M2),
+                lhsT_scale=g_scales[:, u, mc],
+                rhs=x_codes[:, c, ncols].bitcast(E4M3),
+                rhs_scale=x_scales[:, c, ncols],
+                start=start,
+                stop=stop,
+            )
+
+        def new_accs():
+            accs = []
+            for b in range(8):
+                acc = psum.tile([P, HALF], F32, tag="acc%d" % b, name="acc%d" % b)
+                accs.append(acc)
+            return accs
+
+        def leave(eng, acc, h, b):
+            m = 4 * h + b % 4
+            n = b // 4
+            res = stage.tile([P, HALF], F32, tag="res", bufs=8, name="res")
+            if eng == "v":
+                nc.vector.tensor_copy(out=res[:], in_=acc[:])
+            else:
+                nc.scalar.copy(out=res[:], in_=acc[:])
+            nc.sync.dma_start(out=out[m * P : (m + 1) * P, n * HALF : (n + 1) * HALF], in_=res[:])
+
+        emit_loads()
+
+        accs = new_accs()
+        prev_x1 = None
+        for c in range(CHUNKS):
+            graw = raw_tiles[("g", c)]
+            gg = new_grouped()
+            regroup("v", gg[:, 0:G_SPLIT, :], graw[:, :, 0:G_SPLIT])
+            regroup("s", gg[:, G_SPLIT:HALF, :], graw[:, :, G_SPLIT:HALF])
+            state["g_done"] += 1
+            emit_loads()
+            if prev_x1 is not None:
+                quantise_x(prev_x1, c - 1, 1)
+                for m in range(4):
+                    mx_pass(accs[4 + m], c - 1, m, c - 1, 1, c - 1 == 0, False)
+            quantise_g(gg, c)
+            xraw = raw_tiles[("x", c)]
+            gx0 = new_grouped()
+            gx1 = new_grouped()
+            regroup("v", gx0[:], xraw[:, :, 0:HALF])
+            regroup("s", gx1[:], xraw[:, :, HALF : 2 * HALF])
+            state["x_done"] += 1
+            emit_loads()
+            quantise_x(gx0, c, 0)
+            for m in range(4):
+                mx_pass(accs[m], c, m, c, 0, c == 0, c == CHUNKS - 1)
+            prev_x1 = gx1
+
+        grouped_b = {}
+
+        def regroup_b(eng, c):
+            gb = new_grouped()
+            regroup(eng, gb[:], raw_tiles[("g", CHUNKS + c)][:])
+            grouped_b[c] = gb
+
+        regroup_b("v", 0)
+        quantise_x(prev_x1, CHUNKS - 1, 1)
+        for m in range(4):
+            mx_pass(accs[4 + m], CHUNKS - 1, m, CHUNKS - 1, 1, False, True)
+        quantise_g(grouped_b[0], CHUNKS)
+        for b in range(8):
+            leave("s", accs[b], 0, b)
+
+        accs = new_accs()
+
+        def round_two_chunk(c):
+            for b in range(8):
+                mx_pass(accs[b], CHUNKS + c, b % 4, c, b // 4, c == 0, False)
+
+        round_two_chunk(0)
+        regroup_b("v", 1)
+        quantise_g(grouped_b[1], CHUNKS + 1)
+        round_two_chunk(1)
+        regroup_b("v", 2)
+        regroup_b("s", 3)
+        quantise_g(grouped_b[2], CHUNKS + 2)
+        round_two_chunk(2)
+        regroup_b("v", 4)
+        quantise_g(grouped_b[3], CHUNKS + 3)
+        round_two_chunk(3)
+        quantise_g(grouped_b[4], CHUNKS + 4)
+        regroup_b("s", 6)
+        regroup_b("v", 5)
+        quantise_g(grouped_b[5], CHUNKS + 5)
+        regroup_b("v", 7)
+        quantise_g(grouped_b[6], CHUNKS + 6)
+        quantise_g(grouped_b[7], CHUNKS + 7)
+        for b in range(8):
+            for c in range(C_MAJOR, CHUNKS):
+                mx_pass(accs[b], CHUNKS + c, b % 4, c, b // 4, False, c == CHUNKS - 1)
+            leave("s" if b % 2 == 0 else "v", accs[b], 1, b)

@@ -17,6 +17,11 @@ TOKENS = 4096
 CHUNKS = TOKENS // K_PASS
 HALF = 512
 G_SPLIT = 224
+G_SPLIT_LAST = 336
+X0_SPLIT_LAST = 336
+X1_SPLIT_LAST = 208
+H0_SPLIT = 240
+TURN_ENGINES = "sssssvss"
 X_BUFS = 6
 G_BUFS = 8
 C_MAJOR = 4
@@ -121,46 +126,56 @@ def tile_bitlinear_t_kernel(tc, x, weight, grad_out, out):
 
         emit_loads()
 
+        def regroup_split(dst, src, v_cols):
+            if v_cols > 0:
+                regroup("v", dst[:, 0:v_cols, :], src[:, :, 0:v_cols])
+            if v_cols < HALF:
+                regroup("s", dst[:, v_cols:HALF, :], src[:, :, v_cols:HALF])
+
+        def round_one(accs, c, n):
+            for m in range(4):
+                mx_pass(accs[4 * n + m], c, m, c, n, c == 0, c == CHUNKS - 1)
+
         accs = new_accs()
-        prev_x1 = None
+        last = CHUNKS - 1
+        prev = None
         for c in range(CHUNKS):
             graw = raw_tiles[("g", c)]
             gg = new_grouped()
-            regroup("v", gg[:, 0:G_SPLIT, :], graw[:, :, 0:G_SPLIT])
-            regroup("s", gg[:, G_SPLIT:HALF, :], graw[:, :, G_SPLIT:HALF])
+            regroup_split(gg, graw, G_SPLIT if c < last else G_SPLIT_LAST)
             state["g_done"] += 1
             emit_loads()
-            if prev_x1 is not None:
-                quantise_x(prev_x1, c - 1, 1)
-                for m in range(4):
-                    mx_pass(accs[4 + m], c - 1, m, c - 1, 1, c - 1 == 0, False)
+            if prev is not None:
+                quantise_x(prev[0], c - 1, 0)
+                round_one(accs, c - 1, 0)
+                quantise_x(prev[1], c - 1, 1)
+                round_one(accs, c - 1, 1)
             quantise_g(gg, c)
             xraw = raw_tiles[("x", c)]
             gx0 = new_grouped()
             gx1 = new_grouped()
-            regroup("v", gx0[:], xraw[:, :, 0:HALF])
-            regroup("s", gx1[:], xraw[:, :, HALF : 2 * HALF])
+            regroup_split(gx0, xraw[:, :, 0:HALF], HALF if c < last else X0_SPLIT_LAST)
+            regroup_split(gx1, xraw[:, :, HALF : 2 * HALF], 0 if c < last else X1_SPLIT_LAST)
             state["x_done"] += 1
             emit_loads()
-            quantise_x(gx0, c, 0)
-            for m in range(4):
-                mx_pass(accs[m], c, m, c, 0, c == 0, c == CHUNKS - 1)
-            prev_x1 = gx1
+            prev = (gx0, gx1)
+        quantise_x(prev[0], last, 0)
+        round_one(accs, last, 0)
+        quantise_x(prev[1], last, 1)
+        round_one(accs, last, 1)
 
         grouped_b = {}
 
-        def regroup_b(eng, c):
+        def regroup_b(c, v_cols):
             gb = new_grouped()
-            regroup(eng, gb[:], raw_tiles[("g", CHUNKS + c)][:])
+            regroup_split(gb, raw_tiles[("g", CHUNKS + c)], v_cols)
             grouped_b[c] = gb
 
-        regroup_b("v", 0)
-        quantise_x(prev_x1, CHUNKS - 1, 1)
-        for m in range(4):
-            mx_pass(accs[4 + m], CHUNKS - 1, m, CHUNKS - 1, 1, False, True)
+        regroup_b(0, H0_SPLIT)
+        regroup_b(1, HALF)
         quantise_g(grouped_b[0], CHUNKS)
         for b in range(8):
-            leave("s", accs[b], 0, b)
+            leave(TURN_ENGINES[b], accs[b], 0, b)
 
         accs = new_accs()
 
@@ -169,21 +184,20 @@ def tile_bitlinear_t_kernel(tc, x, weight, grad_out, out):
                 mx_pass(accs[b], CHUNKS + c, b % 4, c, b // 4, c == 0, False)
 
         round_two_chunk(0)
-        regroup_b("v", 1)
         quantise_g(grouped_b[1], CHUNKS + 1)
         round_two_chunk(1)
-        regroup_b("v", 2)
-        regroup_b("s", 3)
+        regroup_b(2, HALF)
+        regroup_b(3, 0)
         quantise_g(grouped_b[2], CHUNKS + 2)
         round_two_chunk(2)
-        regroup_b("v", 4)
+        regroup_b(4, HALF)
         quantise_g(grouped_b[3], CHUNKS + 3)
         round_two_chunk(3)
+        regroup_b(5, 0)
         quantise_g(grouped_b[4], CHUNKS + 4)
-        regroup_b("s", 6)
-        regroup_b("v", 5)
+        regroup_b(6, HALF)
         quantise_g(grouped_b[5], CHUNKS + 5)
-        regroup_b("v", 7)
+        regroup_b(7, HALF)
         quantise_g(grouped_b[6], CHUNKS + 6)
         quantise_g(grouped_b[7], CHUNKS + 7)
         for b in range(8):

@@ -34,7 +34,7 @@ def tile_bitlinear_t_kernel(tc, x, weight, grad_out, out):
 
     with tc.tile_pool(name="keep", bufs=1) as keep, tc.tile_pool(name="raw", bufs=1) as raw, tc.tile_pool(
         name="stage", bufs=1
-    ) as stage, tc.psum_pool(name="psum", bufs=1) as psum:
+    ) as stage, tc.psum_pool(name="psum", bufs=1) as psum, tc.manual_schedule():
         x_codes = keep.tile([P, CHUNKS, 2 * HALF], U32, align_bytes=64)
         x_scales = keep.tile([P, CHUNKS, 2 * HALF], U8, align_bytes=64)
         g_codes = keep.tile([P, 2 * CHUNKS, HALF], U32, align_bytes=64)

@@ -17,14 +17,11 @@ TOKENS = 4096
 CHUNKS = TOKENS // K_PASS
 HALF = 512
 G_SPLIT = 224
-G_SPLIT_LAST = 336
-X0_SPLIT_LAST = 336
-X1_SPLIT_LAST = 208
-H0_SPLIT = 240
-TURN_ENGINES = "sssssvss"
+FIRST = 4
+LATE_SPLIT = 256
 X_BUFS = 6
 G_BUFS = 8
-C_MAJOR = 4
+TILE_MAJOR = 2
 
 
 def tile_bitlinear_t_kernel(tc, x, weight, grad_out, out):
@@ -34,18 +31,28 @@ def tile_bitlinear_t_kernel(tc, x, weight, grad_out, out):
 
     with tc.tile_pool(name="keep", bufs=1) as keep, tc.tile_pool(name="raw", bufs=1) as raw, tc.tile_pool(
         name="stage", bufs=1
-    ) as stage, tc.psum_pool(name="psum", bufs=1) as psum, tc.manual_schedule():
+    ) as stage, tc.psum_pool(name="psum", bufs=1) as psum:
         x_codes = keep.tile([P, CHUNKS, 2 * HALF], U32, align_bytes=64)
         x_scales = keep.tile([P, CHUNKS, 2 * HALF], U8, align_bytes=64)
         g_codes = keep.tile([P, 2 * CHUNKS, HALF], U32, align_bytes=64)
         g_scales = keep.tile([P, 2 * CHUNKS, HALF], U8, align_bytes=64)
 
+        part = []
+        for b in range(8):
+            pt = keep.tile([P, HALF], F32, name="part%d" % b)
+            part.append(pt)
+
         order = []
-        for c in range(CHUNKS):
+        for c in range(FIRST):
             order.append(("g", c))
             order.append(("x", c))
-        for c in range(CHUNKS):
+        for c in range(FIRST):
             order.append(("g", CHUNKS + c))
+        for c in range(FIRST, CHUNKS):
+            order.append(("g", CHUNKS + c))
+            order.append(("x", c))
+        for c in range(FIRST, CHUNKS):
+            order.append(("g", c))
         state = {"next": 0, "x_made": 0, "x_done": 0, "g_made": 0, "g_done": 0}
         raw_tiles = {}
 
@@ -114,17 +121,20 @@ def tile_bitlinear_t_kernel(tc, x, weight, grad_out, out):
                 accs.append(acc)
             return accs
 
-        def leave(eng, acc, h, b):
+        def store(res, h, b):
             m = 4 * h + b % 4
             n = b // 4
-            res = stage.tile([P, HALF], F32, tag="res", bufs=8, name="res")
-            if eng == "v":
-                nc.vector.tensor_copy(out=res[:], in_=acc[:])
-            else:
-                nc.scalar.copy(out=res[:], in_=acc[:])
             nc.sync.dma_start(out=out[m * P : (m + 1) * P, n * HALF : (n + 1) * HALF], in_=res[:])
 
-        emit_loads()
+        def copy_out(eng, dst, acc):
+            if eng == "v":
+                nc.vector.tensor_copy(out=dst[:], in_=acc[:])
+            else:
+                nc.scalar.copy(out=dst[:], in_=acc[:])
+
+        def new_res():
+            res = stage.tile([P, HALF], F32, tag="res", bufs=8, name="res")
+            return res
 
         def regroup_split(dst, src, v_cols):
             if v_cols > 0:
@@ -132,75 +142,86 @@ def tile_bitlinear_t_kernel(tc, x, weight, grad_out, out):
             if v_cols < HALF:
                 regroup("s", dst[:, v_cols:HALF, :], src[:, :, v_cols:HALF])
 
-        def round_one(accs, c, n):
-            for m in range(4):
-                mx_pass(accs[4 * n + m], c, m, c, n, c == 0, c == CHUNKS - 1)
-
-        accs = new_accs()
-        last = CHUNKS - 1
-        prev = None
-        for c in range(CHUNKS):
-            graw = raw_tiles[("g", c)]
+        def g_unit(u, v_cols):
             gg = new_grouped()
-            regroup_split(gg, graw, G_SPLIT if c < last else G_SPLIT_LAST)
+            regroup_split(gg, raw_tiles[("g", u)], v_cols)
             state["g_done"] += 1
             emit_loads()
-            if prev is not None:
-                quantise_x(prev[0], c - 1, 0)
-                round_one(accs, c - 1, 0)
-                quantise_x(prev[1], c - 1, 1)
-                round_one(accs, c - 1, 1)
-            quantise_g(gg, c)
+            return gg
+
+        def x_units(c):
             xraw = raw_tiles[("x", c)]
             gx0 = new_grouped()
             gx1 = new_grouped()
-            regroup_split(gx0, xraw[:, :, 0:HALF], HALF if c < last else X0_SPLIT_LAST)
-            regroup_split(gx1, xraw[:, :, HALF : 2 * HALF], 0 if c < last else X1_SPLIT_LAST)
+            regroup_split(gx0, xraw[:, :, 0:HALF], HALF)
+            regroup_split(gx1, xraw[:, :, HALF : 2 * HALF], 0)
             state["x_done"] += 1
             emit_loads()
-            prev = (gx0, gx1)
-        quantise_x(prev[0], last, 0)
-        round_one(accs, last, 0)
-        quantise_x(prev[1], last, 1)
-        round_one(accs, last, 1)
+            return (gx0, gx1)
 
-        grouped_b = {}
+        def passes(accs, h, c, n, start, stop):
+            for m in range(4):
+                mx_pass(accs[4 * n + m], h * CHUNKS + c, m, c, n, start, stop)
 
-        def regroup_b(c, v_cols):
-            gb = new_grouped()
-            regroup_split(gb, raw_tiles[("g", CHUNKS + c)], v_cols)
-            grouped_b[c] = gb
+        def finish_x(accs, h, c, pair, start, stop):
+            for n in range(2):
+                quantise_x(pair[n], c, n)
+                passes(accs, h, c, n, start, stop)
 
-        regroup_b(0, H0_SPLIT)
-        regroup_b(1, HALF)
-        quantise_g(grouped_b[0], CHUNKS)
-        for b in range(8):
-            leave(TURN_ENGINES[b], accs[b], 0, b)
+        emit_loads()
 
         accs = new_accs()
-
-        def round_two_chunk(c):
-            for b in range(8):
-                mx_pass(accs[b], CHUNKS + c, b % 4, c, b // 4, c == 0, False)
-
-        round_two_chunk(0)
-        quantise_g(grouped_b[1], CHUNKS + 1)
-        round_two_chunk(1)
-        regroup_b(2, HALF)
-        regroup_b(3, 0)
-        quantise_g(grouped_b[2], CHUNKS + 2)
-        round_two_chunk(2)
-        regroup_b(4, HALF)
-        quantise_g(grouped_b[3], CHUNKS + 3)
-        round_two_chunk(3)
-        regroup_b(5, 0)
-        quantise_g(grouped_b[4], CHUNKS + 4)
-        regroup_b(6, HALF)
-        quantise_g(grouped_b[5], CHUNKS + 5)
-        regroup_b(7, HALF)
-        quantise_g(grouped_b[6], CHUNKS + 6)
-        quantise_g(grouped_b[7], CHUNKS + 7)
+        prev = None
+        for c in range(FIRST):
+            gg = g_unit(c, G_SPLIT)
+            if prev is not None:
+                finish_x(accs, 0, c - 1, prev, c - 1 == 0, False)
+            quantise_g(gg, c)
+            prev = x_units(c)
+        gg = g_unit(CHUNKS, HALF)
+        finish_x(accs, 0, FIRST - 1, prev, False, True)
+        quantise_g(gg, CHUNKS)
         for b in range(8):
-            for c in range(C_MAJOR, CHUNKS):
-                mx_pass(accs[b], CHUNKS + c, b % 4, c, b // 4, False, c == CHUNKS - 1)
-            leave("s" if b % 2 == 0 else "v", accs[b], 1, b)
+            copy_out("s", part[b], accs[b])
+
+        accs = new_accs()
+        for n in range(2):
+            passes(accs, 1, 0, n, True, False)
+        for c in range(1, FIRST):
+            gg = g_unit(CHUNKS + c, HALF)
+            quantise_g(gg, CHUNKS + c)
+            for n in range(2):
+                passes(accs, 1, c, n, False, False)
+        prev = None
+        for c in range(FIRST, CHUNKS):
+            gg = g_unit(CHUNKS + c, G_SPLIT)
+            if prev is not None:
+                finish_x(accs, 1, c - 1, prev, False, False)
+            quantise_g(gg, CHUNKS + c)
+            prev = x_units(c)
+        gg = g_unit(FIRST, LATE_SPLIT)
+        finish_x(accs, 1, CHUNKS - 1, prev, False, True)
+        quantise_g(gg, FIRST)
+        gg = g_unit(FIRST + 1, LATE_SPLIT)
+        quantise_g(gg, FIRST + 1)
+        for b in range(8):
+            res = new_res()
+            copy_out("s" if b % 2 == 0 else "v", res, accs[b])
+            store(res, 1, b)
+
+        accs = new_accs()
+        for c in range(FIRST, CHUNKS - TILE_MAJOR):
+            if c >= FIRST + 2:
+                gg = g_unit(c, LATE_SPLIT)
+                quantise_g(gg, c)
+            for n in range(2):
+                passes(accs, 0, c, n, c == FIRST, False)
+        for c in range(max(FIRST + 2, CHUNKS - TILE_MAJOR), CHUNKS):
+            gg = g_unit(c, LATE_SPLIT)
+            quantise_g(gg, c)
+        for b in range(8):
+            for c in range(CHUNKS - TILE_MAJOR, CHUNKS):
+                mx_pass(accs[b], c, b % 4, c, b // 4, False, c == CHUNKS - 1)
+            res = new_res()
+            nc.vector.tensor_add(out=res[:], in0=accs[b][:], in1=part[b][:])
+            store(res, 0, b)

@@ -22,6 +22,7 @@ LATE_SPLIT = 256
 X_BUFS = 6
 G_BUFS = 8
 TILE_MAJOR = 2
+RUN = 8
 
 
 def tile_bitlinear_t_kernel(tc, x, weight, grad_out, out):
@@ -78,8 +79,8 @@ def tile_bitlinear_t_kernel(tc, x, weight, grad_out, out):
                 state["next"] += 1
 
         def regroup(eng, dst, src):
-            d = dst.rearrange("p (c i) t -> p c t i", i=4)
-            s = src.rearrange("p t (c i) -> p c t i", i=4)
+            d = dst.rearrange("p (c i) t -> p c t i", i=RUN)
+            s = src.rearrange("p t (c i) -> p c t i", i=RUN)
             if eng == "v":
                 nc.vector.tensor_copy(out=d, in_=s)
             else:

@@ -52,7 +52,7 @@ def tile_bitlinear_t_kernel(tc, x, weight, grad_out, out):
         for c in range(FIRST, CHUNKS):
             order.append(("g", CHUNKS + c))
             order.append(("x", c))
-        for c in range(FIRST, CHUNKS):
+        for c in (FIRST, FIRST + 1, FIRST + 3, FIRST + 2):
             order.append(("g", c))
         state = {"next": 0, "x_made": 0, "x_done": 0, "g_made": 0, "g_done": 0}
         raw_tiles = {}
@@ -179,8 +179,8 @@ def tile_bitlinear_t_kernel(tc, x, weight, grad_out, out):
                 finish_x(accs, 0, c - 1, prev, c - 1 == 0, False)
             quantise_g(gg, c)
             prev = x_units(c)
-        gg = g_unit(CHUNKS, HALF)
         finish_x(accs, 0, FIRST - 1, prev, False, True)
+        gg = g_unit(CHUNKS, HALF)
         quantise_g(gg, CHUNKS)
         for b in range(8):
             copy_out("s", part[b], accs[b])
@@ -200,26 +200,43 @@ def tile_bitlinear_t_kernel(tc, x, weight, grad_out, out):
                 finish_x(accs, 1, c - 1, prev, False, False)
             quantise_g(gg, CHUNKS + c)
             prev = x_units(c)
-        gg = g_unit(FIRST, LATE_SPLIT)
-        finish_x(accs, 1, CHUNKS - 1, prev, False, True)
-        quantise_g(gg, FIRST)
-        gg = g_unit(FIRST + 1, LATE_SPLIT)
-        quantise_g(gg, FIRST + 1)
-        for b in range(8):
-            res = new_res()
-            copy_out("s" if b % 2 == 0 else "v", res, accs[b])
-            store(res, 1, b)
+        def half_accs(n):
+            made = []
+            for m in range(4):
+                acc = psum.tile([P, HALF], F32, tag="acc%d" % (4 * n + m), name="acc%d" % (4 * n + m))
+                made.append(acc)
+            return made
 
-        accs = new_accs()
-        for c in range(FIRST, CHUNKS - TILE_MAJOR):
-            if c >= FIRST + 2:
-                gg = g_unit(c, LATE_SPLIT)
-                quantise_g(gg, c)
-            for n in range(2):
-                passes(accs, 0, c, n, c == FIRST, False)
-        for c in range(max(FIRST + 2, CHUNKS - TILE_MAJOR), CHUNKS):
-            gg = g_unit(c, LATE_SPLIT)
-            quantise_g(gg, c)
+        def empty_half(old, n):
+            for m in range(4):
+                res = new_res()
+                copy_out("s", res, old[4 * n + m])
+                store(res, 1, 4 * n + m)
+
+        old = accs
+        gg = new_grouped()
+        regroup("s", gg[:, LATE_SPLIT:HALF, :], raw_tiles[("g", FIRST)][:, :, LATE_SPLIT:HALF])
+        finish_x(old, 1, CHUNKS - 1, prev, False, True)
+        regroup("v", gg[:, 0:LATE_SPLIT, :], raw_tiles[("g", FIRST)][:, :, 0:LATE_SPLIT])
+        state["g_done"] += 1
+        emit_loads()
+        quantise_g(gg, FIRST)
+        empty_half(old, 0)
+        gg = g_unit(FIRST + 1, HALF)
+        quantise_g(gg, FIRST + 1)
+        accs = half_accs(0)
+        for c in (FIRST, FIRST + 1):
+            for m in range(4):
+                mx_pass(accs[m], c, m, c, 0, c == FIRST, False)
+        empty_half(old, 1)
+        gg = g_unit(FIRST + 3, HALF)
+        quantise_g(gg, FIRST + 3)
+        accs = accs + half_accs(1)
+        for c in (FIRST, FIRST + 1):
+            for m in range(4):
+                mx_pass(accs[4 + m], c, m, c, 1, c == FIRST, False)
+        gg = g_unit(FIRST + 2, LATE_SPLIT)
+        quantise_g(gg, FIRST + 2)
         for b in range(8):
             for c in range(CHUNKS - TILE_MAJOR, CHUNKS):
                 mx_pass(accs[b], c, b % 4, c, b // 4, False, c == CHUNKS - 1)

@@ -16,7 +16,7 @@ K_PASS = P * PACK
 TOKENS = 4096
 CHUNKS = TOKENS // K_PASS
 HALF = 512
-G_SPLIT = 224
+G_SPLIT = 192
 FIRST = 4
 LATE_SPLIT = 256
 X_BUFS = 6
@@ -122,6 +122,13 @@ def tile_bitlinear_t_kernel(tc, x, weight, grad_out, out):
                 accs.append(acc)
             return accs
 
+        def half_accs(n):
+            made = []
+            for m in range(4):
+                acc = psum.tile([P, HALF], F32, tag="acc%d" % (4 * n + m), name="acc%d" % (4 * n + m))
+                made.append(acc)
+            return made
+
         def store(res, h, b):
             m = 4 * h + b % 4
             n = b // 4
@@ -182,13 +189,23 @@ def tile_bitlinear_t_kernel(tc, x, weight, grad_out, out):
         finish_x(accs, 0, FIRST - 1, prev, False, True)
         gg = g_unit(CHUNKS, HALF)
         quantise_g(gg, CHUNKS)
-        for b in range(8):
-            copy_out("s", part[b], accs[b])
 
-        accs = new_accs()
-        for n in range(2):
-            passes(accs, 1, 0, n, True, False)
-        for c in range(1, FIRST):
+        old = accs
+        for b in range(4):
+            copy_out("s", part[b], old[b])
+        gg = g_unit(CHUNKS + 1, HALF)
+        quantise_g(gg, CHUNKS + 1)
+        accs = half_accs(0)
+        for c in range(2):
+            for m in range(4):
+                mx_pass(accs[m], CHUNKS + c, m, c, 0, c == 0, False)
+        for b in range(4, 8):
+            copy_out("s", part[b], old[b])
+        accs = accs + half_accs(1)
+        for c in range(2):
+            for m in range(4):
+                mx_pass(accs[4 + m], CHUNKS + c, m, c, 1, c == 0, False)
+        for c in range(2, FIRST):
             gg = g_unit(CHUNKS + c, HALF)
             quantise_g(gg, CHUNKS + c)
             for n in range(2):
@@ -200,13 +217,6 @@ def tile_bitlinear_t_kernel(tc, x, weight, grad_out, out):
                 finish_x(accs, 1, c - 1, prev, False, False)
             quantise_g(gg, CHUNKS + c)
             prev = x_units(c)
-        def half_accs(n):
-            made = []
-            for m in range(4):
-                acc = psum.tile([P, HALF], F32, tag="acc%d" % (4 * n + m), name="acc%d" % (4 * n + m))
-                made.append(acc)
-            return made
-
         def empty_half(old, n):
             for m in range(4):
                 res = new_res()

@@ -16,13 +16,17 @@ K_PASS = P * PACK
 TOKENS = 4096
 CHUNKS = TOKENS // K_PASS
 HALF = 512
-G_SPLIT = 192
-FIRST = 4
-LATE_SPLIT = 256
+FIRST = 5
+RUN = 8
+G_OWN = 256
+G_OWN2 = 192
+G_EARLY = (256, 512, 512, 512, 512)
+G_TAIL = (256, 256, 512)
+TILE_MAJOR = 2
 X_BUFS = 6
 G_BUFS = 8
-TILE_MAJOR = 2
-RUN = 8
+GROUPED_BUFS = 8
+RES_BUFS = 8
 
 
 def tile_bitlinear_t_kernel(tc, x, weight, grad_out, out):
@@ -37,7 +41,6 @@ def tile_bitlinear_t_kernel(tc, x, weight, grad_out, out):
         x_scales = keep.tile([P, CHUNKS, 2 * HALF], U8, align_bytes=64)
         g_codes = keep.tile([P, 2 * CHUNKS, HALF], U32, align_bytes=64)
         g_scales = keep.tile([P, 2 * CHUNKS, HALF], U8, align_bytes=64)
-
         part = []
         for b in range(8):
             pt = keep.tile([P, HALF], F32, name="part%d" % b)
@@ -52,10 +55,12 @@ def tile_bitlinear_t_kernel(tc, x, weight, grad_out, out):
         for c in range(FIRST, CHUNKS):
             order.append(("g", CHUNKS + c))
             order.append(("x", c))
-        for c in (FIRST, FIRST + 1, FIRST + 3, FIRST + 2):
+        for c in range(FIRST, CHUNKS):
             order.append(("g", c))
         state = {"next": 0, "x_made": 0, "x_done": 0, "g_made": 0, "g_done": 0}
         raw_tiles = {}
+        grouped_tiles = {}
+        banks = {}
 
         def emit_loads():
             while state["next"] < len(order):
@@ -78,6 +83,14 @@ def tile_bitlinear_t_kernel(tc, x, weight, grad_out, out):
                 raw_tiles[(kind, c)] = t
                 state["next"] += 1
 
+        def grouped_of(key):
+            if key not in grouped_tiles:
+                grouped = stage.tile(
+                    [P, HALF, PACK], BF16, tag="grouped", bufs=GROUPED_BUFS, align_bytes=64, name="grouped"
+                )
+                grouped_tiles[key] = grouped
+            return grouped_tiles[key]
+
         def regroup(eng, dst, src):
             d = dst.rearrange("p (c i) t -> p c t i", i=RUN)
             s = src.rearrange("p t (c i) -> p c t i", i=RUN)
@@ -86,27 +99,45 @@ def tile_bitlinear_t_kernel(tc, x, weight, grad_out, out):
             else:
                 nc.scalar.copy(out=d, in_=s)
 
-        def new_grouped():
-            grouped = stage.tile([P, HALF, PACK], BF16, tag="grouped", bufs=6, align_bytes=64, name="grouped")
-            return grouped
+        def g_copy(eng, u, lo, hi):
+            if lo < hi:
+                regroup(eng, grouped_of(("g", u))[:, lo:hi, :], raw_tiles[("g", u)][:, :, lo:hi])
+
+        def g_done():
+            state["g_done"] += 1
+            emit_loads()
+
+        def x_done():
+            state["x_done"] += 1
+            emit_loads()
+
+        def x_copy(eng, c, n):
+            cols = slice(n * HALF, (n + 1) * HALF)
+            regroup(eng, grouped_of(("x", c, n))[:], raw_tiles[("x", c)][:, :, cols])
 
         def quantise(grouped, codes, scales, fmt):
             nc.vector.quantize_mx(
                 out=codes.bitcast(fmt), scales=scales, in_=grouped[:].rearrange("p w j -> p (w j)")
             )
 
-        def quantise_x(grouped, c, n):
+        def q_x(c, n):
             cols = slice(n * HALF, (n + 1) * HALF)
-            quantise(grouped, x_codes[:, c, cols], x_scales[:, c, cols], E4M3)
+            quantise(grouped_of(("x", c, n)), x_codes[:, c, cols], x_scales[:, c, cols], E4M3)
 
-        def quantise_g(grouped, u):
-            quantise(grouped, g_codes[:, u, :], g_scales[:, u, :], E5M2)
+        def q_g(u):
+            quantise(grouped_of(("g", u)), g_codes[:, u, :], g_scales[:, u, :], E5M2)
 
-        def mx_pass(acc, u, m, c, n, start, stop):
+        def open_banks(n):
+            for m in range(4):
+                acc = psum.tile([P, HALF], F32, tag="acc%d" % (4 * n + m), name="acc%d" % (4 * n + m))
+                banks[(n, m)] = acc
+
+        def mx_pass(h, c, n, m, start, stop):
+            u = h * CHUNKS + c
             mc = slice(m * P, (m + 1) * P)
             ncols = slice(n * HALF, (n + 1) * HALF)
             nc.tensor.matmul_mx(
-                out=acc[:],
+                out=banks[(n, m)][:],
                 lhsT=g_codes[:, u, mc].bitcast(E5M2),
                 lhsT_scale=g_scales[:, u, mc],
                 rhs=x_codes[:, c, ncols].bitcast(E4M3),
@@ -115,141 +146,120 @@ def tile_bitlinear_t_kernel(tc, x, weight, grad_out, out):
                 stop=stop,
             )
 
-        def new_accs():
-            accs = []
-            for b in range(8):
-                acc = psum.tile([P, HALF], F32, tag="acc%d" % b, name="acc%d" % b)
-                accs.append(acc)
-            return accs
-
-        def half_accs(n):
-            made = []
+        def passes(h, c, n, start, stop):
             for m in range(4):
-                acc = psum.tile([P, HALF], F32, tag="acc%d" % (4 * n + m), name="acc%d" % (4 * n + m))
-                made.append(acc)
-            return made
+                mx_pass(h, c, n, m, start, stop)
 
-        def store(res, h, b):
-            m = 4 * h + b % 4
-            n = b // 4
-            nc.sync.dma_start(out=out[m * P : (m + 1) * P, n * HALF : (n + 1) * HALF], in_=res[:])
-
-        def copy_out(eng, dst, acc):
+        def park(eng, n, m):
             if eng == "v":
-                nc.vector.tensor_copy(out=dst[:], in_=acc[:])
+                nc.vector.tensor_copy(out=part[4 * n + m][:], in_=banks[(n, m)][:])
             else:
-                nc.scalar.copy(out=dst[:], in_=acc[:])
+                nc.scalar.copy(out=part[4 * n + m][:], in_=banks[(n, m)][:])
 
         def new_res():
-            res = stage.tile([P, HALF], F32, tag="res", bufs=8, name="res")
+            res = stage.tile([P, HALF], F32, tag="res", bufs=RES_BUFS, name="res")
             return res
 
-        def regroup_split(dst, src, v_cols):
-            if v_cols > 0:
-                regroup("v", dst[:, 0:v_cols, :], src[:, :, 0:v_cols])
-            if v_cols < HALF:
-                regroup("s", dst[:, v_cols:HALF, :], src[:, :, v_cols:HALF])
+        def store(res, h, n, m):
+            row = (4 * h + m) * P
+            nc.sync.dma_start(out=out[row : row + P, n * HALF : (n + 1) * HALF], in_=res[:])
 
-        def g_unit(u, v_cols):
-            gg = new_grouped()
-            regroup_split(gg, raw_tiles[("g", u)], v_cols)
-            state["g_done"] += 1
-            emit_loads()
-            return gg
-
-        def x_units(c):
-            xraw = raw_tiles[("x", c)]
-            gx0 = new_grouped()
-            gx1 = new_grouped()
-            regroup_split(gx0, xraw[:, :, 0:HALF], HALF)
-            regroup_split(gx1, xraw[:, :, HALF : 2 * HALF], 0)
-            state["x_done"] += 1
-            emit_loads()
-            return (gx0, gx1)
-
-        def passes(accs, h, c, n, start, stop):
-            for m in range(4):
-                mx_pass(accs[4 * n + m], h * CHUNKS + c, m, c, n, start, stop)
-
-        def finish_x(accs, h, c, pair, start, stop):
-            for n in range(2):
-                quantise_x(pair[n], c, n)
-                passes(accs, h, c, n, start, stop)
-
-        emit_loads()
-
-        accs = new_accs()
-        prev = None
-        for c in range(FIRST):
-            gg = g_unit(c, G_SPLIT)
-            if prev is not None:
-                finish_x(accs, 0, c - 1, prev, c - 1 == 0, False)
-            quantise_g(gg, c)
-            prev = x_units(c)
-        finish_x(accs, 0, FIRST - 1, prev, False, True)
-        gg = g_unit(CHUNKS, HALF)
-        quantise_g(gg, CHUNKS)
-
-        old = accs
-        for b in range(4):
-            copy_out("s", part[b], old[b])
-        gg = g_unit(CHUNKS + 1, HALF)
-        quantise_g(gg, CHUNKS + 1)
-        accs = half_accs(0)
-        for c in range(2):
-            for m in range(4):
-                mx_pass(accs[m], CHUNKS + c, m, c, 0, c == 0, False)
-        for b in range(4, 8):
-            copy_out("s", part[b], old[b])
-        accs = accs + half_accs(1)
-        for c in range(2):
-            for m in range(4):
-                mx_pass(accs[4 + m], CHUNKS + c, m, c, 1, c == 0, False)
-        for c in range(2, FIRST):
-            gg = g_unit(CHUNKS + c, HALF)
-            quantise_g(gg, CHUNKS + c)
-            for n in range(2):
-                passes(accs, 1, c, n, False, False)
-        prev = None
-        for c in range(FIRST, CHUNKS):
-            gg = g_unit(CHUNKS + c, G_SPLIT)
-            if prev is not None:
-                finish_x(accs, 1, c - 1, prev, False, False)
-            quantise_g(gg, CHUNKS + c)
-            prev = x_units(c)
-        def empty_half(old, n):
-            for m in range(4):
-                res = new_res()
-                copy_out("s", res, old[4 * n + m])
-                store(res, 1, 4 * n + m)
-
-        old = accs
-        gg = new_grouped()
-        regroup("s", gg[:, LATE_SPLIT:HALF, :], raw_tiles[("g", FIRST)][:, :, LATE_SPLIT:HALF])
-        finish_x(old, 1, CHUNKS - 1, prev, False, True)
-        regroup("v", gg[:, 0:LATE_SPLIT, :], raw_tiles[("g", FIRST)][:, :, 0:LATE_SPLIT])
-        state["g_done"] += 1
-        emit_loads()
-        quantise_g(gg, FIRST)
-        empty_half(old, 0)
-        gg = g_unit(FIRST + 1, HALF)
-        quantise_g(gg, FIRST + 1)
-        accs = half_accs(0)
-        for c in (FIRST, FIRST + 1):
-            for m in range(4):
-                mx_pass(accs[m], c, m, c, 0, c == FIRST, False)
-        empty_half(old, 1)
-        gg = g_unit(FIRST + 3, HALF)
-        quantise_g(gg, FIRST + 3)
-        accs = accs + half_accs(1)
-        for c in (FIRST, FIRST + 1):
-            for m in range(4):
-                mx_pass(accs[4 + m], c, m, c, 1, c == FIRST, False)
-        gg = g_unit(FIRST + 2, LATE_SPLIT)
-        quantise_g(gg, FIRST + 2)
-        for b in range(8):
-            for c in range(CHUNKS - TILE_MAJOR, CHUNKS):
-                mx_pass(accs[b], c, b % 4, c, b // 4, False, c == CHUNKS - 1)
+        def empty(eng, n, m):
             res = new_res()
-            nc.vector.tensor_add(out=res[:], in0=accs[b][:], in1=part[b][:])
-            store(res, 0, b)
+            if eng == "v":
+                nc.vector.tensor_copy(out=res[:], in_=banks[(n, m)][:])
+            else:
+                nc.scalar.copy(out=res[:], in_=banks[(n, m)][:])
+            store(res, 1, n, m)
+
+        emit_loads()
+
+        open_banks(0)
+        open_banks(1)
+        for c in range(FIRST):
+            g_copy("s", c, G_OWN, HALF)
+            g_copy("v", c, 0, G_OWN)
+            g_done()
+            if c > 0:
+                q_x(c - 1, 1)
+                passes(0, c - 1, 1, c == 1, False)
+            x_copy("s", c, 1)
+            x_copy("v", c, 0)
+            x_done()
+            q_g(c)
+            q_x(c, 0)
+            passes(0, c, 0, c == 0, c == FIRST - 1)
+        def early(i):
+            g_copy("s", CHUNKS + i, G_EARLY[i], HALF)
+            g_copy("v", CHUNKS + i, 0, G_EARLY[i])
+            g_done()
+
+        early(0)
+        q_x(FIRST - 1, 1)
+        passes(0, FIRST - 1, 1, False, True)
+        q_g(CHUNKS)
+        for m in range(4):
+            park("s", 0, m)
+        early(1)
+        open_banks(0)
+        for m in range(4):
+            park("s", 1, m)
+        passes(1, 0, 0, True, False)
+        q_g(CHUNKS + 1)
+        early(2)
+        passes(1, 1, 0, False, False)
+        open_banks(1)
+        for k in range(2):
+            passes(1, k, 1, k == 0, False)
+        for i in range(3, FIRST):
+            early(i)
+            q_g(CHUNKS + i - 1)
+            for n in range(2):
+                passes(1, i - 1, n, False, False)
+        def two(c, n):
+            if c < CHUNKS - TILE_MAJOR:
+                passes(1, c, n, False, False)
+
+        for c in range(FIRST, CHUNKS):
+            u = CHUNKS + c
+            g_copy("s", u, G_OWN2, HALF)
+            g_copy("v", u, 0, G_OWN2)
+            g_done()
+            if c == FIRST:
+                q_g(u - 1)
+                for n in range(2):
+                    two(c - 1, n)
+            else:
+                q_x(c - 1, 1)
+                two(c - 1, 1)
+            x_copy("s", c, 1)
+            x_copy("v", c, 0)
+            x_done()
+            q_g(u)
+            q_x(c, 0)
+            two(c, 0)
+        late = list(range(FIRST, CHUNKS))
+        for i, c in enumerate(late):
+            g_copy("s", c, G_TAIL[i], HALF)
+        g_copy("v", late[0], 0, G_TAIL[0])
+        g_done()
+        q_x(CHUNKS - 1, 1)
+        for n in range(2):
+            for m in range(4):
+                for c in range(CHUNKS - TILE_MAJOR, CHUNKS):
+                    mx_pass(1, c, n, m, False, c == CHUNKS - 1)
+                empty("s", n, m)
+        for i, c in enumerate(late):
+            if i > 0:
+                g_copy("v", c, 0, G_TAIL[i])
+                g_done()
+                q_g(late[i - 1])
+        q_g(late[-1])
+        for n in range(2):
+            open_banks(n)
+            for m in range(4):
+                for c in late:
+                    mx_pass(0, c, n, m, c == FIRST, c == CHUNKS - 1)
+                res = new_res()
+                nc.vector.tensor_add(out=res[:], in0=banks[(n, m)][:], in1=part[4 * n + m][:])
+                store(res, 0, n, m)

import concourse.mybir as mybir

FLOPS = 2 * 4096 * 1024 * 1024
BYTES = 2 * 4096 * 1024 * 2 + 1024 * 1024 * 4

BF16 = mybir.dt.bfloat16
F32 = mybir.dt.float32
U32 = mybir.dt.uint32
U8 = mybir.dt.uint8
E4M3 = mybir.dt.float8_e4m3fn_x4
E5M2 = mybir.dt.float8_e5m2_x4

P = 128
PACK = 4
K_PASS = P * PACK
TOKENS = 4096
CHUNKS = TOKENS // K_PASS
HALF = 512
FIRST = 5
RUN = 8
G_OWN = 256
G_OWN2 = 192
G_EARLY = (256, 512, 512, 512, 512)
G_TAIL = (256, 256, 512)
TILE_MAJOR = 2
X_BUFS = 6
G_BUFS = 8
GROUPED_BUFS = 8
RES_BUFS = 8


def tile_bitlinear_t_kernel(tc, x, weight, grad_out, out):
    nc = tc.nc
    xf = x.flatten_outer_dims()
    gf = grad_out.flatten_outer_dims()

    with tc.tile_pool(name="keep", bufs=1) as keep, tc.tile_pool(name="raw", bufs=1) as raw, tc.tile_pool(
        name="stage", bufs=1
    ) as stage, tc.psum_pool(name="psum", bufs=1) as psum:
        x_codes = keep.tile([P, CHUNKS, 2 * HALF], U32, align_bytes=64)
        x_scales = keep.tile([P, CHUNKS, 2 * HALF], U8, align_bytes=64)
        g_codes = keep.tile([P, 2 * CHUNKS, HALF], U32, align_bytes=64)
        g_scales = keep.tile([P, 2 * CHUNKS, HALF], U8, align_bytes=64)
        part = []
        for b in range(8):
            pt = keep.tile([P, HALF], F32, name="part%d" % b)
            part.append(pt)

        order = []
        for c in range(FIRST):
            order.append(("g", c))
            order.append(("x", c))
        for c in range(FIRST):
            order.append(("g", CHUNKS + c))
        for c in range(FIRST, CHUNKS):
            order.append(("g", CHUNKS + c))
            order.append(("x", c))
        for c in range(FIRST, CHUNKS):
            order.append(("g", c))
        state = {"next": 0, "x_made": 0, "x_done": 0, "g_made": 0, "g_done": 0}
        raw_tiles = {}
        grouped_tiles = {}
        banks = {}

        def emit_loads():
            while state["next"] < len(order):
                kind, c = order[state["next"]]
                if kind == "x":
                    if state["x_made"] - state["x_done"] >= X_BUFS:
                        return
                    t = raw.tile([P, PACK, 2 * HALF], BF16, tag="xraw", bufs=X_BUFS, name="xraw")
                    rows = xf[c * K_PASS : (c + 1) * K_PASS, :]
                    state["x_made"] += 1
                else:
                    if state["g_made"] - state["g_done"] >= G_BUFS:
                        return
                    t = raw.tile([P, PACK, HALF], BF16, tag="graw", bufs=G_BUFS, name="graw")
                    cc = c % CHUNKS
                    h = c // CHUNKS
                    rows = gf[cc * K_PASS : (cc + 1) * K_PASS, h * HALF : (h + 1) * HALF]
                    state["g_made"] += 1
                nc.sync.dma_start(out=t[:], in_=rows.rearrange("(p j) w -> p j w", j=PACK))
                raw_tiles[(kind, c)] = t
                state["next"] += 1

        def grouped_of(key):
            if key not in grouped_tiles:
                grouped = stage.tile(
                    [P, HALF, PACK], BF16, tag="grouped", bufs=GROUPED_BUFS, align_bytes=64, name="grouped"
                )
                grouped_tiles[key] = grouped
            return grouped_tiles[key]

        def regroup(eng, dst, src):
            d = dst.rearrange("p (c i) t -> p c t i", i=RUN)
            s = src.rearrange("p t (c i) -> p c t i", i=RUN)
            if eng == "v":
                nc.vector.tensor_copy(out=d, in_=s)
            else:
                nc.scalar.copy(out=d, in_=s)

        def g_copy(eng, u, lo, hi):
            if lo < hi:
                regroup(eng, grouped_of(("g", u))[:, lo:hi, :], raw_tiles[("g", u)][:, :, lo:hi])

        def g_done():
            state["g_done"] += 1
            emit_loads()

        def x_done():
            state["x_done"] += 1
            emit_loads()

        def x_copy(eng, c, n):
            cols = slice(n * HALF, (n + 1) * HALF)
            regroup(eng, grouped_of(("x", c, n))[:], raw_tiles[("x", c)][:, :, cols])

        def quantise(grouped, codes, scales, fmt):
            nc.vector.quantize_mx(
                out=codes.bitcast(fmt), scales=scales, in_=grouped[:].rearrange("p w j -> p (w j)")
            )

        def q_x(c, n):
            cols = slice(n * HALF, (n + 1) * HALF)
            quantise(grouped_of(("x", c, n)), x_codes[:, c, cols], x_scales[:, c, cols], E4M3)

        def q_g(u):
            quantise(grouped_of(("g", u)), g_codes[:, u, :], g_scales[:, u, :], E5M2)

        def open_banks(n):
            for m in range(4):
                acc = psum.tile([P, HALF], F32, tag="acc%d" % (4 * n + m), name="acc%d" % (4 * n + m))
                banks[(n, m)] = acc

        def mx_pass(h, c, n, m, start, stop):
            u = h * CHUNKS + c
            mc = slice(m * P, (m + 1) * P)
            ncols = slice(n * HALF, (n + 1) * HALF)
            nc.tensor.matmul_mx(
                out=banks[(n, m)][:],
                lhsT=g_codes[:, u, mc].bitcast(E5M2),
                lhsT_scale=g_scales[:, u, mc],
                rhs=x_codes[:, c, ncols].bitcast(E4M3),
                rhs_scale=x_scales[:, c, ncols],
                start=start,
                stop=stop,
            )

        def passes(h, c, n, start, stop):
            for m in range(4):
                mx_pass(h, c, n, m, start, stop)

        def park(eng, n, m):
            if eng == "v":
                nc.vector.tensor_copy(out=part[4 * n + m][:], in_=banks[(n, m)][:])
            else:
                nc.scalar.copy(out=part[4 * n + m][:], in_=banks[(n, m)][:])

        def new_res():
            res = stage.tile([P, HALF], F32, tag="res", bufs=RES_BUFS, name="res")
            return res

        def store(res, h, n, m):
            row = (4 * h + m) * P
            nc.sync.dma_start(out=out[row : row + P, n * HALF : (n + 1) * HALF], in_=res[:])

        def empty(eng, n, m):
            res = new_res()
            if eng == "v":
                nc.vector.tensor_copy(out=res[:], in_=banks[(n, m)][:])
            else:
                nc.scalar.copy(out=res[:], in_=banks[(n, m)][:])
            store(res, 1, n, m)

        emit_loads()

        open_banks(0)
        open_banks(1)
        for c in range(FIRST):
            g_copy("s", c, G_OWN, HALF)
            g_copy("v", c, 0, G_OWN)
            g_done()
            if c > 0:
                q_x(c - 1, 1)
                passes(0, c - 1, 1, c == 1, False)
            x_copy("s", c, 1)
            x_copy("v", c, 0)
            x_done()
            q_g(c)
            q_x(c, 0)
            passes(0, c, 0, c == 0, c == FIRST - 1)
        def early(i):
            g_copy("s", CHUNKS + i, G_EARLY[i], HALF)
            g_copy("v", CHUNKS + i, 0, G_EARLY[i])
            g_done()

        early(0)
        q_x(FIRST - 1, 1)
        passes(0, FIRST - 1, 1, False, True)
        q_g(CHUNKS)
        for m in range(4):
            park("s", 0, m)
        early(1)
        open_banks(0)
        for m in range(4):
            park("s", 1, m)
        passes(1, 0, 0, True, False)
        q_g(CHUNKS + 1)
        early(2)
        passes(1, 1, 0, False, False)
        open_banks(1)
        for k in range(2):
            passes(1, k, 1, k == 0, False)
        for i in range(3, FIRST):
            early(i)
            q_g(CHUNKS + i - 1)
            for n in range(2):
                passes(1, i - 1, n, False, False)
        def two(c, n):
            if c < CHUNKS - TILE_MAJOR:
                passes(1, c, n, False, False)

        for c in range(FIRST, CHUNKS):
            u = CHUNKS + c
            g_copy("s", u, G_OWN2, HALF)
            g_copy("v", u, 0, G_OWN2)
            g_done()
            if c == FIRST:
                q_g(u - 1)
                for n in range(2):
                    two(c - 1, n)
            else:
                q_x(c - 1, 1)
                two(c - 1, 1)
            x_copy("s", c, 1)
            x_copy("v", c, 0)
            x_done()
            q_g(u)
            q_x(c, 0)
            two(c, 0)
        late = list(range(FIRST, CHUNKS))
        for i, c in enumerate(late):
            g_copy("s", c, G_TAIL[i], HALF)
        g_copy("v", late[0], 0, G_TAIL[0])
        g_done()
        q_x(CHUNKS - 1, 1)
        for n in range(2):
            for m in range(4):
                for c in range(CHUNKS - TILE_MAJOR, CHUNKS):
                    mx_pass(1, c, n, m, False, c == CHUNKS - 1)
                empty("s", n, m)
        for i, c in enumerate(late):
            if i > 0:
                g_copy("v", c, 0, G_TAIL[i])
                g_done()
                q_g(late[i - 1])
        q_g(late[-1])
        for n in range(2):
            open_banks(n)
            for m in range(4):
                for c in late:
                    mx_pass(0, c, n, m, c == FIRST, c == CHUNKS - 1)
                res = new_res()
                nc.vector.tensor_add(out=res[:], in0=banks[(n, m)][:], in1=part[4 * n + m][:])
                store(res, 0, n, m)
